import numpy as np
import ml_dtypes


def mxq(x, axis, fmt="e4m3"):
    dtype, down = {"e4m3": (ml_dtypes.float8_e4m3fn, 7), "e5m2": (ml_dtypes.float8_e5m2, 14)}[fmt]
    v = np.moveaxis(np.asarray(x, np.float32).astype(ml_dtypes.bfloat16).astype(np.float64), axis, -1)
    blocks = v.reshape(v.shape[:-1] + (-1, 32))
    amax = np.abs(blocks).max(-1, keepdims=True)
    byte = np.maximum(np.where(amax > 0, np.frexp(amax)[1] - 1 + 127, 0) - down, 1)
    scale = np.exp2(byte - 127.0)
    codes = (blocks / scale).astype(np.float32).astype(dtype).astype(np.float64)
    return np.moveaxis((codes * scale).reshape(v.shape), -1, axis)


WIDE = False


def mx_kscale(k):
    if not WIDE:
        return np.ones(k)
    levels = np.array([10, -10, 5, -5, 0])
    if k % 512:
        return np.exp2(np.random.permutation(np.resize(levels, k // 32))).repeat(32)
    a = np.empty((k // 512, 16))
    for p in range(k // 512):
        a[p, :8] = np.random.permutation(np.resize(levels, 8))
        for g in range(8):
            far = levels[np.abs(levels - a[p, g]) >= 10]
            a[p, g + 8] = far[np.random.randint(len(far))]
    return np.exp2(a.ravel()).repeat(32)


BF16 = ml_dtypes.bfloat16


def bf(x):
    return np.asarray(x, np.float32).astype(BF16)


def f64(x):
    return np.asarray(x).astype(np.float64)


H, I, B = 1024, 1024, 512


def sigmoid(v):
    return 1.0 / (1.0 + np.exp(-v))


def log_sigmoid(v):
    return np.minimum(v, 0.0) - np.log(1.0 + np.exp(-np.abs(v)))


def setup_inputs():
    s, t = mx_kscale(I), mx_kscale(H)

    def w():
        return bf(np.random.standard_normal((H, I)) * 0.7 / np.sqrt(I) / s)

    def r():
        return bf(np.random.standard_normal((H, H)) * 0.7 / np.sqrt(H) / t)

    def b():
        return bf(np.random.standard_normal(H) * 0.3)

    return {"x": bf(np.random.standard_normal((I, B)) * s[:, None]),
            "h_prev": bf(np.random.standard_normal((H, B)) * t[:, None]),
            "c_prev": bf(np.random.standard_normal((H, B))),
            "n_prev": bf(np.random.uniform(size=(H, B))),
            "m_prev": bf(np.random.standard_normal((H, B))),
            "w_input": w(), "w_forget": w(), "w_output": w(), "w_z": w(),
            "r_input": r(), "r_forget": r(), "r_output": r(), "r_z": r(),
            "b_input": b(), "b_forget": b(), "b_output": b(), "b_z": b()}


def reference(x, h_prev, c_prev, n_prev, m_prev,
              w_input, w_forget, w_output, w_z,
              r_input, r_forget, r_output, r_z,
              b_input, b_forget, b_output, b_z):
    xq = mxq(f64(x), 0, "e4m3")
    hq = mxq(f64(h_prev), 0, "e4m3")
    input_wave = (mxq(f64(w_input), 1, "e4m3") @ xq) + (mxq(f64(r_input), 1, "e4m3") @ hq) + f64(b_input)[:, None]
    forget_wave = (mxq(f64(w_forget), 1, "e4m3") @ xq) + (mxq(f64(r_forget), 1, "e4m3") @ hq) + f64(b_forget)[:, None]
    output_wave = (mxq(f64(w_output), 1, "e4m3") @ xq) + (mxq(f64(r_output), 1, "e4m3") @ hq) + f64(b_output)[:, None]
    z_wave = (mxq(f64(w_z), 1, "e4m3") @ xq) + (mxq(f64(r_z), 1, "e4m3") @ hq) + f64(b_z)[:, None]

    log_i = input_wave
    log_f = log_sigmoid(forget_wave)
    m_t = np.maximum(log_f + f64(m_prev), log_i)
    input_prime = np.exp(log_i - m_t)
    forget_prime = np.exp(log_f + f64(m_prev) - m_t)

    c_t = forget_prime * f64(c_prev) + input_prime * np.tanh(z_wave)
    n_t = forget_prime * f64(n_prev) + forget_prime
    h_wave = c_t / n_t
    h_t = sigmoid(output_wave) * np.tanh(h_wave)
    return (h_t, c_t, n_t, m_t)

@@ -1,0 +1,331 @@
+from contextlib import ExitStack
+
+import concourse.mybir as mybir
+from concourse.masks import make_identity
+
+F32 = mybir.dt.float32
+BF16 = mybir.dt.bfloat16
+U32 = mybir.dt.uint32
+U8 = mybir.dt.uint8
+FP8X4 = mybir.dt.float8_e4m3fn_x4
+ACT = mybir.ActivationFunctionType
+ALU = mybir.AluOpType
+
+P = 128
+FEATURES = 1024
+BATCH = 512
+TILES = FEATURES // P
+PAIRS = TILES // 2
+PACK = 4
+PASSES = FEATURES // (P * PACK)
+WORDS = FEATURES // 2
+GATES = 4
+FORGET, INPUT, CELL, OUTPUT = range(GATES)
+UNITS = GATES * TILES
+
+FLOPS = 2 * 2 * GATES * FEATURES * FEATURES * BATCH
+
+AT_FORGET = FORGET * TILES + 1
+AT_INPUT = INPUT * TILES + 1
+AT_CELL = CELL * TILES + 1
+AT_OUTPUT = OUTPUT * TILES + 1
+AT_LOGS = AT_FORGET + TILES - 1
+AT_SPAN = AT_INPUT + 1
+AT_EXP = AT_LOGS + PAIRS
+AT_NORM = AT_OUTPUT - 4
+
+RAW_AHEAD = 10
+VECTOR_COLUMNS = 336
+
+
+def tile_slstmcell_pa_kernel(
+    tc, x, h_prev, c_prev, n_prev, m_prev,
+    w_input, w_forget, w_output, w_z, r_input, r_forget, r_output, r_z,
+    b_input, b_forget, b_output, b_z,
+    out_0, out_1, out_2, out_3,
+):
+    nc = tc.nc
+    w_of = (w_forget, w_input, w_z, w_output)
+    r_of = (r_forget, r_input, r_z, r_output)
+    b_of = (b_forget, b_input, b_z, b_output)
+
+    def by_tile(a):
+        return a.rearrange("(p t) c -> p t c", t=TILES)
+
+    h_out, c_out, n_out, m_out = by_tile(out_0), by_tile(out_1), by_tile(out_2), by_tile(out_3)
+
+    with ExitStack() as ctx:
+        ctx.enter_context(tc.manual_schedule())
+        consts = ctx.enter_context(tc.tile_pool(name="consts", bufs=1))
+        raw_pool = ctx.enter_context(tc.tile_pool(name="raw", bufs=RAW_AHEAD))
+        grouped_pool = ctx.enter_context(tc.tile_pool(name="grouped", bufs=3))
+        codes_pool = ctx.enter_context(tc.tile_pool(name="codes", bufs=3))
+        state = ctx.enter_context(tc.tile_pool(name="state", bufs=PAIRS))
+        temps = ctx.enter_context(tc.tile_pool(name="temps", bufs=2))
+        results = ctx.enter_context(tc.tile_pool(name="results", bufs=2))
+        turned_pool = ctx.enter_context(tc.psum_pool(name="turned", bufs=4))
+        wave_pool = ctx.enter_context(tc.psum_pool(name="waves", bufs=4))
+
+        identity = consts.tile([P, P], F32, name="identity")
+        make_identity(nc, identity[:])
+        bias_bf = consts.tile([P, GATES, 2 * TILES], BF16, name="bias_bf")
+        for gate in range(GATES):
+            nc.scalar.dma_start(out=bias_bf[:, gate, 0:TILES], in_=b_of[gate].rearrange("(p t) -> p t", t=TILES))
+
+        moving_codes = consts.tile([P, 2 * PASSES, BATCH], U32, name="moving_codes", align_bytes=64)
+        moving_scales = consts.tile([P, 2 * PASSES, BATCH], U8, name="moving_scales", align_bytes=64)
+        m_old = consts.tile([P, TILES, BATCH], BF16, name="m_old")
+        n_old = consts.tile([P, TILES, BATCH], BF16, name="n_old")
+        c_old = consts.tile([P, TILES, BATCH], BF16, name="c_old")
+
+        moving_raw = []
+        for source in (x, h_prev):
+            passes = source.rearrange("(g q t) b -> q g t b", g=PASSES, t=PACK)
+            for g in range(PASSES):
+                raw = raw_pool.tile([P, PACK, BATCH], BF16, tag="raw", name="moving_raw%d" % len(moving_raw))
+                nc.sync.dma_start(out=raw[:], in_=passes[:, g])
+                moving_raw.append(raw)
+
+        raw_of = {}
+
+        def load_pair(pair):
+            gate, first = divmod(2 * pair, TILES)
+            for m, matrix in enumerate((w_of[gate], r_of[gate])):
+                raw = raw_pool.tile([P, 2, FEATURES], BF16, tag="raw", name="raw%d_%d" % (pair, m))
+                nc.sync.dma_start(out=raw[:], in_=by_tile(matrix)[:, first : first + 2, :])
+                raw_of[(pair, m)] = raw
+            if gate == FORGET:
+                nc.sync.dma_start(out=m_old[:, first : first + 2, :], in_=by_tile(m_prev)[:, first : first + 2, :])
+            if pair == PAIRS - 1:
+                nc.sync.dma_start(out=n_old[:], in_=by_tile(n_prev))
+            if pair == PAIRS + 1:
+                nc.sync.dma_start(out=c_old[:], in_=by_tile(c_prev))
+
+        pairs_at_once = (RAW_AHEAD - len(moving_raw)) // 2
+        for pair in range(pairs_at_once):
+            load_pair(pair)
+
+        moving_grouped = []
+        for j in range(2 * PASSES + 1):
+            if j < 2 * PASSES:
+                grouped = grouped_pool.tile([P, BATCH, PACK], BF16, tag="grouped", name="moving_grouped%d" % j, align_bytes=64)
+                moving_grouped.append(grouped)
+                for engine_copy, cols in ((nc.vector.tensor_copy, slice(0, VECTOR_COLUMNS)), (nc.scalar.copy, slice(VECTOR_COLUMNS, BATCH))):
+                    engine_copy(
+                        out=grouped[:, cols, :].rearrange("p (c i) t -> p c t i", i=4),
+                        in_=moving_raw[j][:, :, cols].rearrange("p t (c i) -> p c t i", i=4),
+                    )
+            if j > 0:
+                nc.vector.quantize_mx(
+                    out=moving_codes[:, j - 1, :].bitcast(FP8X4),
+                    scales=moving_scales[:, j - 1, :],
+                    in_=moving_grouped[j - 1][:].rearrange("p b t -> p (b t)"),
+                )
+
+        one = consts.tile([P, 1], F32, name="one")
+        nc.vector.memset(one[:], 1.0)
+        bias = consts.tile([P, GATES, TILES], F32, name="bias")
+        nc.vector.tensor_copy(out=bias[:], in_=bias_bf[:, :, 0:TILES])
+        minus_bias_f = consts.tile([P, TILES], F32, name="minus_bias_f")
+        nc.vector.tensor_scalar(out=minus_bias_f[:], in0=bias[:, FORGET, :], scalar1=-1.0, scalar2=None, op0=ALU.mult)
+        half_bias_o = consts.tile([P, TILES], F32, name="half_bias_o")
+        nc.vector.tensor_scalar(out=half_bias_o[:], in0=bias[:, OUTPUT, :], scalar1=0.5, scalar2=None, op0=ALU.mult)
+
+        def column(table, t):
+            return table[:, t : t + 1]
+
+        banks_of, grouped_of, codes_of, scales_of, wave_of = {}, {}, {}, {}, {}
+
+        def turn(u):
+            for m in range(2):
+                words = raw_of[(u // 2, m)][:, u % 2, :].bitcast(F32)
+                bank = turned_pool.tile([P, 2 * PASSES, P], F32, tag="turned", name="turned%d_%d" % (u, m))
+                for c in range(2 * PASSES):
+                    first = 2 * P * (c // 2) + c % 2
+                    nc.tensor.transpose(bank[:, c, :], words[:, first : 2 * P * (c // 2 + 1) : 2], identity[:])
+                banks_of[(u, m)] = bank
+
+        def evacuate(u, m, engine_copy):
+            if u not in grouped_of:
+                grouped_of[u] = grouped_pool.tile([P, 2 * FEATURES], BF16, tag="grouped", name="grouped%d" % u, align_bytes=64)
+            words = grouped_of[u][:].bitcast(F32)[:, m * WORDS : (m + 1) * WORDS]
+            engine_copy(
+                out=words.rearrange("p (g h u) -> p g h u", g=PASSES, u=2),
+                in_=banks_of[(u, m)][:].rearrange("p (g u) h -> p g h u", u=2),
+            )
+
+        def quantise(u):
+            codes_of[u] = codes_pool.tile([P, 2 * PASSES * P], U32, tag="codes", name="codes%d" % u, align_bytes=64)
+            scales_of[u] = codes_pool.tile([P, 2 * PASSES * P], U8, tag="scales", name="scales%d" % u, align_bytes=64)
+            nc.vector.quantize_mx(out=codes_of[u][:].bitcast(FP8X4), scales=scales_of[u][:], in_=grouped_of[u][:])
+
+        def multiply(u):
+            wave_of[u] = wave_pool.tile([P, BATCH], F32, tag="wave", name="wave%d" % u)
+            for j in range(2 * PASSES):
+                cols = slice(j * P, (j + 1) * P)
+                nc.tensor.matmul_mx(
+                    out=wave_of[u][:],
+                    lhsT=codes_of[u][:, cols].bitcast(FP8X4),
+                    lhsT_scale=scales_of[u][:, cols],
+                    rhs=moving_codes[:, j, :].bitcast(FP8X4),
+                    rhs_scale=moving_scales[:, j, :],
+                    start=(j == 0),
+                    stop=(j == 2 * PASSES - 1),
+                )
+
+        m_plus_b, soft, log_fm, log_n1, gap, span, c_new, shrink, z_part, h_wave, h_new, m_new = ({} for k in range(12))
+
+        def pair_tile(pool, tag, j):
+            return pool.tile([P, 2, BATCH], F32, tag=tag, name="%s%d" % (tag, j))
+
+        def rows(j):
+            return slice(2 * j, 2 * j + 2)
+
+        def s_magnitude(t):
+            if t % 2 == 0:
+                soft[t // 2] = pair_tile(state, "soft_gap", t // 2)
+            nc.scalar.activation(out=soft[t // 2][:, t % 2, :], in_=wave_of[t][:], func=ACT.Abs, bias=column(bias[:, FORGET, :], t), scale=1.0)
+
+        def v_floor(t):
+            if t % 2 == 0:
+                log_fm[t // 2] = pair_tile(state, "log_fm_h", t // 2)
+            nc.vector.scalar_tensor_tensor(
+                out=log_fm[t // 2][:, t % 2, :], in0=wave_of[t][:], scalar=column(minus_bias_f, t), in1=m_plus_b[t // 2][:, t % 2, :],
+                op0=ALU.min, op1=ALU.add,
+            )
+
+        def v_input(t):
+            wave = wave_of[INPUT * TILES + t]
+            if t % 2 == 0:
+                gap[t // 2] = pair_tile(state, "soft_gap", PAIRS + t // 2)
+                m_new[t // 2] = pair_tile(results, "m_new", t // 2)
+            for out, op1 in ((gap[t // 2], ALU.subtract), (m_new[t // 2], ALU.max)):
+                nc.vector.scalar_tensor_tensor(
+                    out=out[:, t % 2, :], in0=wave[:], scalar=column(bias[:, INPUT, :], t), in1=log_fm[t // 2][:, t % 2, :],
+                    op0=ALU.add, op1=op1,
+                )
+            if t % 2 == 1:
+                nc.sync.dma_start(out=m_out[:, rows(t // 2), :], in_=m_new[t // 2][:])
+
+        def s_cell(t):
+            if t % 2 == 0:
+                z_part[t // 2] = pair_tile(temps, "z_part", t // 2)
+            nc.scalar.activation(out=z_part[t // 2][:, t % 2, :], in_=wave_of[CELL * TILES + t][:], func=ACT.Tanh, bias=column(bias[:, CELL, :], t), scale=1.0)
+
+        def s_output(t):
+            h_new[t] = results.tile([P, BATCH], F32, tag="h_new", name="h_new%d" % t, bufs=4)
+            nc.scalar.activation(out=h_new[t][:], in_=wave_of[OUTPUT * TILES + t][:], func=ACT.Tanh, bias=column(half_bias_o, t), scale=0.5)
+
+        def v_h_new(t):
+            nc.vector.scalar_tensor_tensor(out=h_new[t][:], in0=h_new[t][:], scalar=1.0, in1=h_wave[t // 2][:, t % 2, :], op0=ALU.add, op1=ALU.mult)
+            nc.sync.dma_start(out=h_out[:, t, :], in_=h_new[t][:])
+
+        def v_m_plus_b(j):
+            m_plus_b[j] = pair_tile(temps, "m_plus_b", j)
+            for t in (2 * j, 2 * j + 1):
+                nc.vector.tensor_scalar(out=m_plus_b[j][:, t % 2, :], in0=m_old[:, t, :], scalar1=column(bias[:, FORGET, :], t), scalar2=None, op0=ALU.add)
+
+        def s_decay(j):
+            nc.scalar.activation(out=soft[j][:], in_=soft[j][:], func=ACT.Exp, scale=-1.0)
+
+        def s_logs(j):
+            nc.scalar.activation(out=soft[j][:], in_=soft[j][:], func=ACT.Ln, bias=one[:], scale=1.0)
+            log_n1[j] = pair_tile(state, "log_n1_c", j)
+            nc.scalar.activation(out=log_n1[j][:], in_=n_old[:, rows(j), :], func=ACT.Ln, bias=one[:], scale=1.0)
+
+        def v_log_fm(j):
+            nc.vector.tensor_tensor(out=log_fm[j][:], in0=log_fm[j][:], in1=soft[j][:], op=ALU.subtract)
+
+        def v_span(j):
+            span[j] = pair_tile(state, "span", j)
+            nc.vector.scalar_tensor_tensor(out=span[j][:], in0=gap[j][:], scalar=0.0, in1=log_n1[j][:], op0=ALU.max, op1=ALU.subtract)
+
+        def s_ratios(j):
+            shrink[j] = pair_tile(temps, "shrink", j)
+            nc.scalar.activation(out=shrink[j][:], in_=gap[j][:], func=ACT.Exp, scale=-1.0)
+            nc.scalar.activation(out=gap[j][:], in_=gap[j][:], func=ACT.Exp, scale=1.0)
+
+        def v_old_part(j):
+            c_new[j] = pair_tile(state, "log_n1_c", PAIRS + j)
+            nc.vector.scalar_tensor_tensor(out=c_new[j][:], in0=shrink[j][:], scalar=1.0, in1=c_old[:, rows(j), :], op0=ALU.min, op1=ALU.mult)
+
+        def v_new_part(j):
+            nc.vector.scalar_tensor_tensor(out=z_part[j][:], in0=gap[j][:], scalar=1.0, in1=z_part[j][:], op0=ALU.min, op1=ALU.mult)
+
+        def v_c_new(j):
+            nc.vector.tensor_tensor(out=c_new[j][:], in0=c_new[j][:], in1=z_part[j][:], op=ALU.add)
+            nc.sync.dma_start(out=c_out[:, rows(j), :], in_=c_new[j][:])
+
+        def s_norm(j):
+            n_new = pair_tile(results, "n_new", j)
+            nc.scalar.activation(out=n_new[:], in_=span[j][:], func=ACT.Exp, scale=-1.0)
+            nc.sync.dma_start(out=n_out[:, rows(j), :], in_=n_new[:])
+            nc.scalar.activation(out=span[j][:], in_=span[j][:], func=ACT.Exp, scale=1.0)
+
+        def v_h_wave(j):
+            h_wave[j] = pair_tile(state, "log_fm_h", PAIRS + j)
+            nc.vector.tensor_tensor(out=h_wave[j][:], in0=c_new[j][:], in1=span[j][:], op=ALU.mult)
+
+        def s_squash(j):
+            nc.scalar.activation(out=h_wave[j][:], in_=h_wave[j][:], func=ACT.Tanh, scale=1.0)
+
+        def v_halve(j):
+            nc.vector.tensor_scalar(out=h_wave[j][:], in0=h_wave[j][:], scalar1=0.5, scalar2=None, op0=ALU.mult)
+
+        def at(step, t):
+            if 0 <= t < TILES:
+                step(t)
+
+        def at_pair(step, t):
+            if 0 <= t < TILES and t % 2 == 1:
+                step(t // 2)
+
+        def at_each_pair(step, j):
+            if 0 <= j < PAIRS:
+                step(j)
+
+        for s in range(-3, UNITS + 2):
+            if s % 2 == 0 and pairs_at_once <= s // 2 + pairs_at_once + 1 < UNITS // 2:
+                load_pair(s // 2 + pairs_at_once + 1)
+
+            if 0 <= s < UNITS:
+                multiply(s)
+            if 0 <= s + 3 < UNITS:
+                turn(s + 3)
+
+            emptied = s + 2
+            gate, tile_in_gate = divmod(emptied, TILES)
+            vector_takes = []
+            if 0 <= s - AT_LOGS < PAIRS - 1:
+                vector_takes.append(0)
+            if gate in (FORGET, OUTPUT) or (gate == INPUT and tile_in_gate < PAIRS):
+                vector_takes.append(1)
+
+            at(s_magnitude, s - AT_FORGET)
+            for m in range(2):
+                if 0 <= emptied < UNITS and m not in vector_takes:
+                    evacuate(emptied, m, nc.scalar.copy)
+            at_pair(s_decay, s - AT_FORGET)
+            at(s_cell, s - AT_CELL)
+            at(s_output, s - AT_OUTPUT)
+            at_each_pair(s_logs, s - AT_LOGS)
+            at_pair(s_ratios, s - AT_EXP)
+            at_pair(s_norm, s - AT_NORM)
+            at_pair(s_squash, s - AT_NORM - 2)
+
+            at(v_h_new, s - AT_OUTPUT - 1)
+            at_pair(v_new_part, s - AT_CELL - 1)
+            if 0 <= s + 1 < UNITS:
+                quantise(s + 1)
+            at_pair(v_span, s - AT_SPAN)
+            at_pair(v_old_part, s - AT_EXP - 1)
+            at_pair(v_c_new, s - AT_CELL - 1)
+            at_pair(v_halve, s - AT_NORM - 3)
+            at_pair(v_h_wave, s - AT_NORM - 1)
+            at_pair(v_m_plus_b, s + 2)
+            for m in range(2):
+                if 0 <= emptied < UNITS and m in vector_takes:
+                    evacuate(emptied, m, nc.vector.tensor_copy)
+            at(v_floor, s - AT_FORGET)
+            at_each_pair(v_log_fm, s - AT_LOGS - 1)
+            at(v_input, s - AT_INPUT)

@@ -1,3 +1,4 @@
+import math
 from contextlib import ExitStack
 
 import concourse.mybir as mybir
@@ -29,10 +30,20 @@ AT_FORGET = FORGET * TILES + 1
 AT_INPUT = INPUT * TILES + 1
 AT_CELL = CELL * TILES + 1
 AT_OUTPUT = OUTPUT * TILES + 1
+AT_SIGMOID = 3
+AT_INV_N1 = AT_SIGMOID + 1
 AT_LOGS = AT_FORGET + TILES - 1
-AT_SPAN = AT_INPUT + 1
-AT_EXP = AT_LOGS + PAIRS
-AT_NORM = AT_OUTPUT - 4
+AT_GROW = AT_LOGS + PAIRS
+AT_N_NEW = AT_GROW + 2
+AT_PRODUCT = AT_CELL + 2
+AT_H_WAVE = AT_PRODUCT + 2
+
+FLOOR = -16.0
+TINY = 2.0**-100
+FIRST_SHARED = 5
+LAST_SHARED = 11
+CEILING = 80.0
+GROWTH_CEILING = math.exp(CEILING)
 
 RAW_AHEAD = 10
 VECTOR_COLUMNS = 336
@@ -61,7 +72,6 @@ def tile_slstmcell_pa_kernel(
         grouped_pool = ctx.enter_context(tc.tile_pool(name="grouped", bufs=3))
         codes_pool = ctx.enter_context(tc.tile_pool(name="codes", bufs=3))
         state = ctx.enter_context(tc.tile_pool(name="state", bufs=PAIRS))
-        temps = ctx.enter_context(tc.tile_pool(name="temps", bufs=2))
         results = ctx.enter_context(tc.tile_pool(name="results", bufs=2))
         turned_pool = ctx.enter_context(tc.psum_pool(name="turned", bufs=4))
         wave_pool = ctx.enter_context(tc.psum_pool(name="waves", bufs=4))
@@ -78,14 +88,6 @@ def tile_slstmcell_pa_kernel(
         n_old = consts.tile([P, TILES, BATCH], BF16, name="n_old")
         c_old = consts.tile([P, TILES, BATCH], BF16, name="c_old")
 
-        moving_raw = []
-        for source in (x, h_prev):
-            passes = source.rearrange("(g q t) b -> q g t b", g=PASSES, t=PACK)
-            for g in range(PASSES):
-                raw = raw_pool.tile([P, PACK, BATCH], BF16, tag="raw", name="moving_raw%d" % len(moving_raw))
-                nc.sync.dma_start(out=raw[:], in_=passes[:, g])
-                moving_raw.append(raw)
-
         raw_of = {}
 
         def load_pair(pair):
@@ -96,43 +98,56 @@ def tile_slstmcell_pa_kernel(
                 raw_of[(pair, m)] = raw
             if gate == FORGET:
                 nc.sync.dma_start(out=m_old[:, first : first + 2, :], in_=by_tile(m_prev)[:, first : first + 2, :])
-            if pair == PAIRS - 1:
+            if pair == 1:
                 nc.sync.dma_start(out=n_old[:], in_=by_tile(n_prev))
             if pair == PAIRS + 1:
                 nc.sync.dma_start(out=c_old[:], in_=by_tile(c_prev))
 
+        moving_raw = []
+
+        def load_moving(source):
+            passes = source.rearrange("(g q t) b -> q g t b", g=PASSES, t=PACK)
+            for g in range(PASSES):
+                raw = raw_pool.tile([P, PACK, BATCH], BF16, tag="raw", name="moving_raw%d" % len(moving_raw))
+                nc.sync.dma_start(out=raw[:], in_=passes[:, g])
+                moving_raw.append(raw)
+
+        load_pair(0)
+        load_moving(x)
+        load_moving(h_prev)
         pairs_at_once = (RAW_AHEAD - len(moving_raw)) // 2
-        for pair in range(pairs_at_once):
+        for pair in range(1, pairs_at_once):
             load_pair(pair)
 
         moving_grouped = []
-        for j in range(2 * PASSES + 1):
-            if j < 2 * PASSES:
-                grouped = grouped_pool.tile([P, BATCH, PACK], BF16, tag="grouped", name="moving_grouped%d" % j, align_bytes=64)
-                moving_grouped.append(grouped)
-                for engine_copy, cols in ((nc.vector.tensor_copy, slice(0, VECTOR_COLUMNS)), (nc.scalar.copy, slice(VECTOR_COLUMNS, BATCH))):
-                    engine_copy(
-                        out=grouped[:, cols, :].rearrange("p (c i) t -> p c t i", i=4),
-                        in_=moving_raw[j][:, :, cols].rearrange("p t (c i) -> p c t i", i=4),
-                    )
-            if j > 0:
-                nc.vector.quantize_mx(
-                    out=moving_codes[:, j - 1, :].bitcast(FP8X4),
-                    scales=moving_scales[:, j - 1, :],
-                    in_=moving_grouped[j - 1][:].rearrange("p b t -> p (b t)"),
+
+        def regroup_moving(j):
+            grouped = grouped_pool.tile([P, BATCH, PACK], BF16, tag="grouped", name="moving_grouped%d" % j, align_bytes=64)
+            moving_grouped.append(grouped)
+            for engine_copy, cols in ((nc.vector.tensor_copy, slice(0, VECTOR_COLUMNS)), (nc.scalar.copy, slice(VECTOR_COLUMNS, BATCH))):
+                engine_copy(
+                    out=grouped[:, cols, :].rearrange("p (c i) t -> p c t i", i=4),
+                    in_=moving_raw[j][:, :, cols].rearrange("p t (c i) -> p c t i", i=4),
                 )
 
-        one = consts.tile([P, 1], F32, name="one")
-        nc.vector.memset(one[:], 1.0)
-        bias = consts.tile([P, GATES, TILES], F32, name="bias")
-        nc.vector.tensor_copy(out=bias[:], in_=bias_bf[:, :, 0:TILES])
-        minus_bias_f = consts.tile([P, TILES], F32, name="minus_bias_f")
-        nc.vector.tensor_scalar(out=minus_bias_f[:], in0=bias[:, FORGET, :], scalar1=-1.0, scalar2=None, op0=ALU.mult)
-        half_bias_o = consts.tile([P, TILES], F32, name="half_bias_o")
-        nc.vector.tensor_scalar(out=half_bias_o[:], in0=bias[:, OUTPUT, :], scalar1=0.5, scalar2=None, op0=ALU.mult)
+        def quantise_moving(j):
+            nc.vector.quantize_mx(
+                out=moving_codes[:, j, :].bitcast(FP8X4),
+                scales=moving_scales[:, j, :],
+                in_=moving_grouped[j][:].rearrange("p b t -> p (b t)"),
+            )
 
         def column(table, t):
             return table[:, t : t + 1]
+
+        tiny = consts.tile([P, 1], F32, name="tiny")
+        bias = consts.tile([P, GATES, TILES], F32, name="bias")
+        edge = consts.tile([P, TILES], F32, name="edge")
+
+        def make_constants():
+            nc.vector.memset(tiny[:], TINY)
+            nc.vector.tensor_copy(out=bias[:], in_=bias_bf[:, :, 0:TILES])
+            nc.vector.tensor_scalar(out=edge[:], in0=bias[:, FORGET, :], scalar1=FLOOR, scalar2=None, op0=ALU.add)
 
         banks_of, grouped_of, codes_of, scales_of, wave_of = {}, {}, {}, {}, {}
 
@@ -173,7 +188,7 @@ def tile_slstmcell_pa_kernel(
                     stop=(j == 2 * PASSES - 1),
                 )
 
-        m_plus_b, soft, log_fm, log_n1, gap, span, c_new, shrink, z_part, h_wave, h_new, m_new = ({} for k in range(12))
+        log_f, log_fm, inv_n1, gap, rise, total, h_wave, h_new, m_new = ({} for k in range(9))
 
         def pair_tile(pool, tag, j):
             return pool.tile([P, 2, BATCH], F32, tag=tag, name="%s%d" % (tag, j))
@@ -181,23 +196,22 @@ def tile_slstmcell_pa_kernel(
         def rows(j):
             return slice(2 * j, 2 * j + 2)
 
-        def s_magnitude(t):
+        def s_forget(t):
             if t % 2 == 0:
-                soft[t // 2] = pair_tile(state, "soft_gap", t // 2)
-            nc.scalar.activation(out=soft[t // 2][:, t % 2, :], in_=wave_of[t][:], func=ACT.Abs, bias=column(bias[:, FORGET, :], t), scale=1.0)
+                log_f[t // 2] = pair_tile(state, "log_f_gap", t // 2)
+            nc.scalar.activation(out=log_f[t // 2][:, t % 2, :], in_=wave_of[t][:], func=ACT.Sigmoid, bias=column(bias[:, FORGET, :], t), scale=1.0)
 
         def v_floor(t):
             if t % 2 == 0:
                 log_fm[t // 2] = pair_tile(state, "log_fm_h", t // 2)
             nc.vector.scalar_tensor_tensor(
-                out=log_fm[t // 2][:, t % 2, :], in0=wave_of[t][:], scalar=column(minus_bias_f, t), in1=m_plus_b[t // 2][:, t % 2, :],
-                op0=ALU.min, op1=ALU.add,
+                out=log_fm[t // 2][:, t % 2, :], in0=wave_of[t][:], scalar=FLOOR, in1=m_old[:, t, :], op0=ALU.min, op1=ALU.add
             )
 
         def v_input(t):
             wave = wave_of[INPUT * TILES + t]
             if t % 2 == 0:
-                gap[t // 2] = pair_tile(state, "soft_gap", PAIRS + t // 2)
+                gap[t // 2] = pair_tile(state, "log_f_gap", PAIRS + t // 2)
                 m_new[t // 2] = pair_tile(results, "m_new", t // 2)
             for out, op1 in ((gap[t // 2], ALU.subtract), (m_new[t // 2], ALU.max)):
                 nc.vector.scalar_tensor_tensor(
@@ -209,123 +223,151 @@ def tile_slstmcell_pa_kernel(
 
         def s_cell(t):
             if t % 2 == 0:
-                z_part[t // 2] = pair_tile(temps, "z_part", t // 2)
-            nc.scalar.activation(out=z_part[t // 2][:, t % 2, :], in_=wave_of[CELL * TILES + t][:], func=ACT.Tanh, bias=column(bias[:, CELL, :], t), scale=1.0)
+                total[t // 2] = pair_tile(state, "total", t // 2)
+            nc.scalar.activation(out=total[t // 2][:, t % 2, :], in_=wave_of[CELL * TILES + t][:], func=ACT.Tanh, bias=column(bias[:, CELL, :], t), scale=1.0)
 
         def s_output(t):
             h_new[t] = results.tile([P, BATCH], F32, tag="h_new", name="h_new%d" % t, bufs=4)
-            nc.scalar.activation(out=h_new[t][:], in_=wave_of[OUTPUT * TILES + t][:], func=ACT.Tanh, bias=column(half_bias_o, t), scale=0.5)
+            nc.scalar.activation(out=h_new[t][:], in_=wave_of[OUTPUT * TILES + t][:], func=ACT.Sigmoid, bias=column(bias[:, OUTPUT, :], t), scale=1.0)
 
         def v_h_new(t):
-            nc.vector.scalar_tensor_tensor(out=h_new[t][:], in0=h_new[t][:], scalar=1.0, in1=h_wave[t // 2][:, t % 2, :], op0=ALU.add, op1=ALU.mult)
+            nc.vector.tensor_tensor(out=h_new[t][:], in0=h_new[t][:], in1=h_wave[t // 2][:, t % 2, :], op=ALU.mult)
             nc.sync.dma_start(out=h_out[:, t, :], in_=h_new[t][:])
 
-        def v_m_plus_b(j):
-            m_plus_b[j] = pair_tile(temps, "m_plus_b", j)
-            for t in (2 * j, 2 * j + 1):
-                nc.vector.tensor_scalar(out=m_plus_b[j][:, t % 2, :], in0=m_old[:, t, :], scalar1=column(bias[:, FORGET, :], t), scalar2=None, op0=ALU.add)
+        def s_log_n(j):
+            inv_n1[j] = pair_tile(state, "inv_n1", j)
+            nc.scalar.activation(out=inv_n1[j][:], in_=n_old[:, rows(j), :], func=ACT.Ln, bias=tiny[:], scale=1.0)
 
-        def s_decay(j):
-            nc.scalar.activation(out=soft[j][:], in_=soft[j][:], func=ACT.Exp, scale=-1.0)
+        def s_inv_n1(j):
+            nc.scalar.activation(out=inv_n1[j][:], in_=inv_n1[j][:], func=ACT.Sigmoid, scale=-1.0)
+
+        def s_edge():
+            nc.scalar.activation(out=edge[:], in_=edge[:], func=ACT.Sigmoid, scale=1.0)
 
         def s_logs(j):
-            nc.scalar.activation(out=soft[j][:], in_=soft[j][:], func=ACT.Ln, bias=one[:], scale=1.0)
-            log_n1[j] = pair_tile(state, "log_n1_c", j)
-            nc.scalar.activation(out=log_n1[j][:], in_=n_old[:, rows(j), :], func=ACT.Ln, bias=one[:], scale=1.0)
+            if j == 0:
+                nc.scalar.activation(out=edge[:], in_=edge[:], func=ACT.Ln, scale=math.exp(-FLOOR))
+            nc.scalar.activation(out=log_f[j][:], in_=log_f[j][:], func=ACT.Ln, scale=math.exp(-FLOOR))
 
         def v_log_fm(j):
-            nc.vector.tensor_tensor(out=log_fm[j][:], in0=log_fm[j][:], in1=soft[j][:], op=ALU.subtract)
+            for t in (2 * j, 2 * j + 1):
+                half = log_fm[j][:, t % 2, :]
+                nc.vector.scalar_tensor_tensor(
+                    out=half, in0=log_f[j][:, t % 2, :], scalar=column(edge, t), in1=half, op0=ALU.max, op1=ALU.add
+                )
 
-        def v_span(j):
-            span[j] = pair_tile(state, "span", j)
-            nc.vector.scalar_tensor_tensor(out=span[j][:], in0=gap[j][:], scalar=0.0, in1=log_n1[j][:], op0=ALU.max, op1=ALU.subtract)
+        def v_rise(j):
+            rise[j] = pair_tile(state, "rise", j)
+            nc.vector.tensor_scalar(out=rise[j][:], in0=gap[j][:], scalar1=0.0, scalar2=CEILING, op0=ALU.max, op1=ALU.min)
 
-        def s_ratios(j):
-            shrink[j] = pair_tile(temps, "shrink", j)
-            nc.scalar.activation(out=shrink[j][:], in_=gap[j][:], func=ACT.Exp, scale=-1.0)
+        def s_grow(j):
             nc.scalar.activation(out=gap[j][:], in_=gap[j][:], func=ACT.Exp, scale=1.0)
 
-        def v_old_part(j):
-            c_new[j] = pair_tile(state, "log_n1_c", PAIRS + j)
-            nc.vector.scalar_tensor_tensor(out=c_new[j][:], in0=shrink[j][:], scalar=1.0, in1=c_old[:, rows(j), :], op0=ALU.min, op1=ALU.mult)
+        def s_keep(j):
+            nc.scalar.activation(out=rise[j][:], in_=rise[j][:], func=ACT.Exp, scale=-1.0)
 
-        def v_new_part(j):
-            nc.vector.scalar_tensor_tensor(out=z_part[j][:], in0=gap[j][:], scalar=1.0, in1=z_part[j][:], op0=ALU.min, op1=ALU.mult)
-
-        def v_c_new(j):
-            nc.vector.tensor_tensor(out=c_new[j][:], in0=c_new[j][:], in1=z_part[j][:], op=ALU.add)
-            nc.sync.dma_start(out=c_out[:, rows(j), :], in_=c_new[j][:])
-
-        def s_norm(j):
+        def v_n_new(j):
             n_new = pair_tile(results, "n_new", j)
-            nc.scalar.activation(out=n_new[:], in_=span[j][:], func=ACT.Exp, scale=-1.0)
+            nc.vector.scalar_tensor_tensor(out=n_new[:], in0=n_old[:, rows(j), :], scalar=1.0, in1=rise[j][:], op0=ALU.add, op1=ALU.mult)
             nc.sync.dma_start(out=n_out[:, rows(j), :], in_=n_new[:])
-            nc.scalar.activation(out=span[j][:], in_=span[j][:], func=ACT.Exp, scale=1.0)
+
+        def v_product(j):
+            nc.vector.scalar_tensor_tensor(out=total[j][:], in0=gap[j][:], scalar=GROWTH_CEILING, in1=total[j][:], op0=ALU.min, op1=ALU.mult)
+
+        def v_total(j):
+            nc.vector.tensor_tensor(out=total[j][:], in0=total[j][:], in1=c_old[:, rows(j), :], op=ALU.add)
 
         def v_h_wave(j):
             h_wave[j] = pair_tile(state, "log_fm_h", PAIRS + j)
-            nc.vector.tensor_tensor(out=h_wave[j][:], in0=c_new[j][:], in1=span[j][:], op=ALU.mult)
+            nc.vector.tensor_tensor(out=h_wave[j][:], in0=total[j][:], in1=inv_n1[j][:], op=ALU.mult)
+
+        def v_c_new(j):
+            c_new = pair_tile(results, "c_new", j)
+            nc.vector.tensor_tensor(out=c_new[:], in0=total[j][:], in1=rise[j][:], op=ALU.mult)
+            nc.sync.dma_start(out=c_out[:, rows(j), :], in_=c_new[:])
 
         def s_squash(j):
             nc.scalar.activation(out=h_wave[j][:], in_=h_wave[j][:], func=ACT.Tanh, scale=1.0)
-
-        def v_halve(j):
-            nc.vector.tensor_scalar(out=h_wave[j][:], in0=h_wave[j][:], scalar1=0.5, scalar2=None, op0=ALU.mult)
 
         def at(step, t):
             if 0 <= t < TILES:
                 step(t)
 
         def at_pair(step, t):
-            if 0 <= t < TILES and t % 2 == 1:
+            if 0 <= t < TILES and t % 2 == 0:
                 step(t // 2)
 
         def at_each_pair(step, j):
             if 0 <= j < PAIRS:
                 step(j)
 
-        for s in range(-3, UNITS + 2):
-            if s % 2 == 0 and pairs_at_once <= s // 2 + pairs_at_once + 1 < UNITS // 2:
-                load_pair(s // 2 + pairs_at_once + 1)
+        turn(0)
+        turn(1)
+        evacuate(0, 0, nc.scalar.copy)
+        evacuate(0, 1, nc.vector.tensor_copy)
+        make_constants()
+        regroup_moving(0)
+        quantise(0)
+        evacuate(1, 0, nc.scalar.copy)
+        regroup_moving(1)
+        quantise_moving(0)
+        evacuate(1, 1, nc.vector.tensor_copy)
+        turn(2)
+        regroup_moving(2)
+        quantise_moving(1)
+        regroup_moving(3)
+        quantise_moving(2)
+        quantise_moving(3)
 
-            if 0 <= s < UNITS:
+        for s in range(UNITS + 2):
+            if s % 2 == 0 and s // 2 + pairs_at_once < UNITS // 2:
+                load_pair(s // 2 + pairs_at_once)
+
+            if s < UNITS:
                 multiply(s)
-            if 0 <= s + 3 < UNITS:
+            if s + 3 < UNITS:
                 turn(s + 3)
 
             emptied = s + 2
-            gate, tile_in_gate = divmod(emptied, TILES)
-            vector_takes = []
-            if 0 <= s - AT_LOGS < PAIRS - 1:
-                vector_takes.append(0)
-            if gate in (FORGET, OUTPUT) or (gate == INPUT and tile_in_gate < PAIRS):
-                vector_takes.append(1)
+            if emptied < FIRST_SHARED or AT_LOGS + 2 <= emptied < LAST_SHARED:
+                vector_takes = (0, 1)
+            elif emptied < AT_LOGS + 2:
+                vector_takes = (1,)
+            else:
+                vector_takes = ()
 
-            at(s_magnitude, s - AT_FORGET)
+            at(v_floor, s - AT_FORGET)
+
             for m in range(2):
-                if 0 <= emptied < UNITS and m not in vector_takes:
+                if emptied < UNITS and m not in vector_takes:
                     evacuate(emptied, m, nc.scalar.copy)
-            at_pair(s_decay, s - AT_FORGET)
+            if s in (0, 1):
+                s_log_n(2 * s)
+                s_log_n(2 * s + 1)
+            at_each_pair(s_inv_n1, s - AT_INV_N1)
             at(s_cell, s - AT_CELL)
             at(s_output, s - AT_OUTPUT)
+            if s == AT_LOGS - 1:
+                s_edge()
+            for t in range(TILES):
+                if s == max(t + AT_FORGET, AT_SIGMOID):
+                    s_forget(t)
             at_each_pair(s_logs, s - AT_LOGS)
-            at_pair(s_ratios, s - AT_EXP)
-            at_pair(s_norm, s - AT_NORM)
-            at_pair(s_squash, s - AT_NORM - 2)
+            at_pair(s_grow, s - AT_GROW)
+            at_pair(s_keep, s - AT_GROW - 1)
+            at_pair(s_squash, s - AT_H_WAVE - 1)
 
             at(v_h_new, s - AT_OUTPUT - 1)
-            at_pair(v_new_part, s - AT_CELL - 1)
-            if 0 <= s + 1 < UNITS:
+            if s + 1 < UNITS:
                 quantise(s + 1)
-            at_pair(v_span, s - AT_SPAN)
-            at_pair(v_old_part, s - AT_EXP - 1)
-            at_pair(v_c_new, s - AT_CELL - 1)
-            at_pair(v_halve, s - AT_NORM - 3)
-            at_pair(v_h_wave, s - AT_NORM - 1)
-            at_pair(v_m_plus_b, s + 2)
+            at_pair(v_n_new, s - AT_N_NEW)
+            at_pair(v_h_wave, s - AT_H_WAVE)
+            at_pair(v_product, s - AT_PRODUCT)
+            at_pair(v_rise, s - AT_INPUT - 2)
+            at_pair(v_log_fm, s - AT_INPUT)
             for m in range(2):
-                if 0 <= emptied < UNITS and m in vector_takes:
+                if emptied < UNITS and m in vector_takes:
                     evacuate(emptied, m, nc.vector.tensor_copy)
-            at(v_floor, s - AT_FORGET)
-            at_each_pair(v_log_fm, s - AT_LOGS - 1)
+            at_pair(v_total, s - AT_PRODUCT - 1)
+            at_pair(v_c_new, s - AT_H_WAVE - 3)
             at(v_input, s - AT_INPUT)

@@ -30,7 +30,7 @@ AT_FORGET = FORGET * TILES + 1
 AT_INPUT = INPUT * TILES + 1
 AT_CELL = CELL * TILES + 1
 AT_OUTPUT = OUTPUT * TILES + 1
-AT_SIGMOID = 3
+AT_SIGMOID = 2
 AT_INV_N1 = AT_SIGMOID + 1
 AT_LOGS = AT_FORGET + TILES - 1
 AT_GROW = AT_LOGS + PAIRS
@@ -40,7 +40,7 @@ AT_H_WAVE = AT_PRODUCT + 2
 
 FLOOR = -16.0
 TINY = 2.0**-100
-FIRST_SHARED = 5
+FIRST_SHARED = 6
 LAST_SHARED = 11
 CEILING = 80.0
 GROWTH_CEILING = math.exp(CEILING)
@@ -90,34 +90,46 @@ def tile_slstmcell_pa_kernel(
 
         raw_of = {}
 
-        def load_pair(pair):
+        def load_rows(pair, rows):
             gate, first = divmod(2 * pair, TILES)
             for m, matrix in enumerate((w_of[gate], r_of[gate])):
-                raw = raw_pool.tile([P, 2, FEATURES], BF16, tag="raw", name="raw%d_%d" % (pair, m))
-                nc.sync.dma_start(out=raw[:], in_=by_tile(matrix)[:, first : first + 2, :])
-                raw_of[(pair, m)] = raw
+                if (pair, m) not in raw_of:
+                    raw_of[(pair, m)] = raw_pool.tile([P, 2, FEATURES], BF16, tag="raw", name="raw%d_%d" % (pair, m))
+                nc.sync.dma_start(out=raw_of[(pair, m)][:, rows, :], in_=by_tile(matrix)[:, first + rows.start : first + rows.stop, :])
+
+        def load_pair(pair):
+            load_rows(pair, slice(0, 2))
+            load_old(pair)
+
+        def load_old(pair):
+            gate, first = divmod(2 * pair, TILES)
             if gate == FORGET:
                 nc.sync.dma_start(out=m_old[:, first : first + 2, :], in_=by_tile(m_prev)[:, first : first + 2, :])
-            if pair == 1:
-                nc.sync.dma_start(out=n_old[:], in_=by_tile(n_prev))
             if pair == PAIRS + 1:
                 nc.sync.dma_start(out=c_old[:], in_=by_tile(c_prev))
 
-        moving_raw = []
+        moving_raw = {}
 
-        def load_moving(source):
-            passes = source.rearrange("(g q t) b -> q g t b", g=PASSES, t=PACK)
-            for g in range(PASSES):
-                raw = raw_pool.tile([P, PACK, BATCH], BF16, tag="raw", name="moving_raw%d" % len(moving_raw))
-                nc.sync.dma_start(out=raw[:], in_=passes[:, g])
-                moving_raw.append(raw)
+        def load_moving(j):
+            source, g = ((x, h_prev)[j // PASSES], j % PASSES)
+            moving_raw[j] = raw_pool.tile([P, PACK, BATCH], BF16, tag="raw", name="moving_raw%d" % j)
+            nc.sync.dma_start(out=moving_raw[j][:], in_=source.rearrange("(g q t) b -> q g t b", g=PASSES, t=PACK)[:, g])
 
-        load_pair(0)
-        load_moving(x)
-        load_moving(h_prev)
-        pairs_at_once = (RAW_AHEAD - len(moving_raw)) // 2
-        for pair in range(1, pairs_at_once):
-            load_pair(pair)
+        def load_n(j):
+            nc.sync.dma_start(out=n_old[:, 4 * j : 4 * j + 4, :], in_=by_tile(n_prev)[:, 4 * j : 4 * j + 4, :])
+
+        load_moving(0)
+        load_rows(0, slice(0, 1))
+        load_moving(1)
+        load_moving(2)
+        load_moving(3)
+        load_rows(0, slice(1, 2))
+        load_old(0)
+        load_n(0)
+        load_pair(1)
+        load_n(1)
+        load_pair(2)
+        pairs_at_once = (RAW_AHEAD - 2 * PASSES) // 2
 
         moving_grouped = []
 
@@ -301,23 +313,22 @@ def tile_slstmcell_pa_kernel(
             if 0 <= j < PAIRS:
                 step(j)
 
-        turn(0)
-        turn(1)
-        evacuate(0, 0, nc.scalar.copy)
-        evacuate(0, 1, nc.vector.tensor_copy)
         make_constants()
         regroup_moving(0)
-        quantise(0)
-        evacuate(1, 0, nc.scalar.copy)
-        regroup_moving(1)
+        turn(0)
         quantise_moving(0)
-        evacuate(1, 1, nc.vector.tensor_copy)
-        turn(2)
-        regroup_moving(2)
+        evacuate(0, 0, nc.scalar.copy)
+        evacuate(0, 1, nc.scalar.copy)
+        regroup_moving(1)
+        quantise(0)
         quantise_moving(1)
-        regroup_moving(3)
+        regroup_moving(2)
+        turn(1)
         quantise_moving(2)
+        regroup_moving(3)
+        evacuate(1, 0, nc.scalar.copy)
         quantise_moving(3)
+        evacuate(1, 1, nc.scalar.copy)
 
         for s in range(UNITS + 2):
             if s % 2 == 0 and s // 2 + pairs_at_once < UNITS // 2:
@@ -325,6 +336,8 @@ def tile_slstmcell_pa_kernel(
 
             if s < UNITS:
                 multiply(s)
+            if s == 0:
+                turn(2)
             if s + 3 < UNITS:
                 turn(s + 3)
 

@@ -129,7 +129,7 @@ def tile_slstmcell_pa_kernel(
         load_pair(1)
         load_n(1)
         load_pair(2)
-        pairs_at_once = (RAW_AHEAD - 2 * PASSES) // 2
+        pairs_at_first = (RAW_AHEAD - 2 * PASSES) // 2
 
         moving_grouped = []
 
@@ -153,11 +153,13 @@ def tile_slstmcell_pa_kernel(
             return table[:, t : t + 1]
 
         tiny = consts.tile([P, 1], F32, name="tiny")
+        nc.gpsimd.memset(tiny[:], TINY)
+        first_log = consts.tile([P, 1], F32, name="first_log")
+        nc.scalar.activation(out=first_log[:], in_=tiny[:], func=ACT.Ln, bias=tiny[:], scale=1.0)
         bias = consts.tile([P, GATES, TILES], F32, name="bias")
         edge = consts.tile([P, TILES], F32, name="edge")
 
         def make_constants():
-            nc.vector.memset(tiny[:], TINY)
             nc.vector.tensor_copy(out=bias[:], in_=bias_bf[:, :, 0:TILES])
             nc.vector.tensor_scalar(out=edge[:], in0=bias[:, FORGET, :], scalar1=FLOOR, scalar2=None, op0=ALU.add)
 
@@ -313,7 +315,6 @@ def tile_slstmcell_pa_kernel(
             if 0 <= j < PAIRS:
                 step(j)
 
-        make_constants()
         regroup_moving(0)
         turn(0)
         quantise_moving(0)
@@ -321,6 +322,7 @@ def tile_slstmcell_pa_kernel(
         evacuate(0, 1, nc.scalar.copy)
         regroup_moving(1)
         quantise(0)
+        make_constants()
         quantise_moving(1)
         regroup_moving(2)
         turn(1)
@@ -331,8 +333,11 @@ def tile_slstmcell_pa_kernel(
         evacuate(1, 1, nc.scalar.copy)
 
         for s in range(UNITS + 2):
-            if s % 2 == 0 and s // 2 + pairs_at_once < UNITS // 2:
-                load_pair(s // 2 + pairs_at_once)
+            if s == 0:
+                for pair in range(pairs_at_first, RAW_AHEAD // 2 + 1):
+                    load_pair(pair)
+            elif s % 2 == 0 and s // 2 + RAW_AHEAD // 2 < UNITS // 2:
+                load_pair(s // 2 + RAW_AHEAD // 2)
 
             if s < UNITS:
                 multiply(s)

@@ -11,6 +11,7 @@ U8 = mybir.dt.uint8
 FP8X4 = mybir.dt.float8_e4m3fn_x4
 ACT = mybir.ActivationFunctionType
 ALU = mybir.AluOpType
+ET = mybir.EngineType
 
 P = 128
 FEATURES = 1024
@@ -34,7 +35,7 @@ AT_SIGMOID = 2
 AT_INV_N1 = AT_SIGMOID + 1
 AT_LOGS = AT_FORGET + TILES - 1
 AT_GROW = AT_LOGS + PAIRS
-AT_N_NEW = AT_GROW + 2
+AT_N_NEW = AT_GROW + 4
 AT_PRODUCT = AT_CELL + 2
 AT_H_WAVE = AT_PRODUCT + 2
 
@@ -66,7 +67,7 @@ def tile_slstmcell_pa_kernel(
     h_out, c_out, n_out, m_out = by_tile(out_0), by_tile(out_1), by_tile(out_2), by_tile(out_3)
 
     with ExitStack() as ctx:
-        ctx.enter_context(tc.manual_schedule())
+        ctx.enter_context(tc.manual_schedule(engines={ET.PE, ET.SP, ET.Activation}))
         consts = ctx.enter_context(tc.tile_pool(name="consts", bufs=1))
         raw_pool = ctx.enter_context(tc.tile_pool(name="raw", bufs=RAW_AHEAD))
         grouped_pool = ctx.enter_context(tc.tile_pool(name="grouped", bufs=3))
@@ -165,6 +166,10 @@ def tile_slstmcell_pa_kernel(
 
         banks_of, grouped_of, codes_of, scales_of, wave_of = {}, {}, {}, {}, {}
 
+        def parts_of(u):
+            n = 2 if u == UNITS - 1 else 1
+            return [slice(i * BATCH // n, (i + 1) * BATCH // n) for i in range(n)]
+
         def turn(u):
             for m in range(2):
                 words = raw_of[(u // 2, m)][:, u % 2, :].bitcast(F32)
@@ -190,17 +195,18 @@ def tile_slstmcell_pa_kernel(
 
         def multiply(u):
             wave_of[u] = wave_pool.tile([P, BATCH], F32, tag="wave", name="wave%d" % u)
-            for j in range(2 * PASSES):
-                cols = slice(j * P, (j + 1) * P)
-                nc.tensor.matmul_mx(
-                    out=wave_of[u][:],
-                    lhsT=codes_of[u][:, cols].bitcast(FP8X4),
-                    lhsT_scale=scales_of[u][:, cols],
-                    rhs=moving_codes[:, j, :].bitcast(FP8X4),
-                    rhs_scale=moving_scales[:, j, :],
-                    start=(j == 0),
-                    stop=(j == 2 * PASSES - 1),
-                )
+            for part in parts_of(u):
+                for j in range(2 * PASSES):
+                    cols = slice(j * P, (j + 1) * P)
+                    nc.tensor.matmul_mx(
+                        out=wave_of[u][:, part],
+                        lhsT=codes_of[u][:, cols].bitcast(FP8X4),
+                        lhsT_scale=scales_of[u][:, cols],
+                        rhs=moving_codes[:, j, part].bitcast(FP8X4),
+                        rhs_scale=moving_scales[:, j, part],
+                        start=(j == 0),
+                        stop=(j == 2 * PASSES - 1),
+                    )
 
         log_f, log_fm, inv_n1, gap, rise, total, h_wave, h_new, m_new = ({} for k in range(9))
 
@@ -242,11 +248,13 @@ def tile_slstmcell_pa_kernel(
 
         def s_output(t):
             h_new[t] = results.tile([P, BATCH], F32, tag="h_new", name="h_new%d" % t, bufs=4)
-            nc.scalar.activation(out=h_new[t][:], in_=wave_of[OUTPUT * TILES + t][:], func=ACT.Sigmoid, bias=column(bias[:, OUTPUT, :], t), scale=1.0)
+            for part in parts_of(OUTPUT * TILES + t):
+                nc.scalar.activation(out=h_new[t][:, part], in_=wave_of[OUTPUT * TILES + t][:, part], func=ACT.Sigmoid, bias=column(bias[:, OUTPUT, :], t), scale=1.0)
 
         def v_h_new(t):
-            nc.vector.tensor_tensor(out=h_new[t][:], in0=h_new[t][:], in1=h_wave[t // 2][:, t % 2, :], op=ALU.mult)
-            nc.sync.dma_start(out=h_out[:, t, :], in_=h_new[t][:])
+            for part in parts_of(OUTPUT * TILES + t):
+                nc.vector.tensor_tensor(out=h_new[t][:, part], in0=h_new[t][:, part], in1=h_wave[t // 2][:, t % 2, part], op=ALU.mult)
+                nc.sync.dma_start(out=h_out[:, t, part], in_=h_new[t][:, part])
 
         def s_log_n(j):
             inv_n1[j] = pair_tile(state, "inv_n1", j)
@@ -387,5 +395,5 @@ def tile_slstmcell_pa_kernel(
                 if emptied < UNITS and m in vector_takes:
                     evacuate(emptied, m, nc.vector.tensor_copy)
             at_pair(v_total, s - AT_PRODUCT - 1)
-            at_pair(v_c_new, s - AT_H_WAVE - 3)
+            at_pair(v_c_new, s - AT_H_WAVE - 2)
             at(v_input, s - AT_INPUT)

@@ -41,8 +41,8 @@ AT_H_WAVE = AT_PRODUCT + 2
 
 FLOOR = -16.0
 TINY = 2.0**-100
-FIRST_SHARED = 6
-LAST_SHARED = 11
+AHEAD_FROM = TILES - 1
+SCALAR_EMPTIES = 11
 CEILING = 80.0
 GROWTH_CEILING = math.exp(CEILING)
 
@@ -102,10 +102,13 @@ def tile_slstmcell_pa_kernel(
             load_rows(pair, slice(0, 2))
             load_old(pair)
 
+        def load_m(pair):
+            nc.sync.dma_start(out=m_old[:, 2 * pair : 2 * pair + 2, :], in_=by_tile(m_prev)[:, 2 * pair : 2 * pair + 2, :])
+
         def load_old(pair):
             gate, first = divmod(2 * pair, TILES)
-            if gate == FORGET:
-                nc.sync.dma_start(out=m_old[:, first : first + 2, :], in_=by_tile(m_prev)[:, first : first + 2, :])
+            if gate == FORGET and pair >= 3:
+                load_m(pair)
             if pair == PAIRS + 1:
                 nc.sync.dma_start(out=c_old[:], in_=by_tile(c_prev))
 
@@ -125,11 +128,13 @@ def tile_slstmcell_pa_kernel(
         load_moving(2)
         load_moving(3)
         load_rows(0, slice(1, 2))
-        load_old(0)
+        load_rows(1, slice(0, 2))
         load_n(0)
-        load_pair(1)
+        load_m(0)
         load_n(1)
-        load_pair(2)
+        load_rows(2, slice(0, 2))
+        load_m(1)
+        load_m(2)
         pairs_at_first = (RAW_AHEAD - 2 * PASSES) // 2
 
         moving_grouped = []
@@ -157,12 +162,9 @@ def tile_slstmcell_pa_kernel(
         nc.gpsimd.memset(tiny[:], TINY)
         first_log = consts.tile([P, 1], F32, name="first_log")
         nc.scalar.activation(out=first_log[:], in_=tiny[:], func=ACT.Ln, bias=tiny[:], scale=1.0)
-        bias = consts.tile([P, GATES, TILES], F32, name="bias")
+        floor = consts.tile([P, 1], F32, name="floor")
+        nc.gpsimd.memset(floor[:], FLOOR)
         edge = consts.tile([P, TILES], F32, name="edge")
-
-        def make_constants():
-            nc.vector.tensor_copy(out=bias[:], in_=bias_bf[:, :, 0:TILES])
-            nc.vector.tensor_scalar(out=edge[:], in0=bias[:, FORGET, :], scalar1=FLOOR, scalar2=None, op0=ALU.add)
 
         banks_of, grouped_of, codes_of, scales_of, wave_of = {}, {}, {}, {}, {}
 
@@ -219,7 +221,7 @@ def tile_slstmcell_pa_kernel(
         def s_forget(t):
             if t % 2 == 0:
                 log_f[t // 2] = pair_tile(state, "log_f_gap", t // 2)
-            nc.scalar.activation(out=log_f[t // 2][:, t % 2, :], in_=wave_of[t][:], func=ACT.Sigmoid, bias=column(bias[:, FORGET, :], t), scale=1.0)
+            nc.scalar.activation(out=log_f[t // 2][:, t % 2, :], in_=wave_of[t][:], func=ACT.Sigmoid, bias=column(bias_bf[:, FORGET, :], t), scale=1.0)
 
         def v_floor(t):
             if t % 2 == 0:
@@ -235,7 +237,7 @@ def tile_slstmcell_pa_kernel(
                 m_new[t // 2] = pair_tile(results, "m_new", t // 2)
             for out, op1 in ((gap[t // 2], ALU.subtract), (m_new[t // 2], ALU.max)):
                 nc.vector.scalar_tensor_tensor(
-                    out=out[:, t % 2, :], in0=wave[:], scalar=column(bias[:, INPUT, :], t), in1=log_fm[t // 2][:, t % 2, :],
+                    out=out[:, t % 2, :], in0=wave[:], scalar=column(bias_bf[:, INPUT, :], t), in1=log_fm[t // 2][:, t % 2, :],
                     op0=ALU.add, op1=op1,
                 )
             if t % 2 == 1:
@@ -244,12 +246,12 @@ def tile_slstmcell_pa_kernel(
         def s_cell(t):
             if t % 2 == 0:
                 total[t // 2] = pair_tile(state, "total", t // 2)
-            nc.scalar.activation(out=total[t // 2][:, t % 2, :], in_=wave_of[CELL * TILES + t][:], func=ACT.Tanh, bias=column(bias[:, CELL, :], t), scale=1.0)
+            nc.scalar.activation(out=total[t // 2][:, t % 2, :], in_=wave_of[CELL * TILES + t][:], func=ACT.Tanh, bias=column(bias_bf[:, CELL, :], t), scale=1.0)
 
         def s_output(t):
             h_new[t] = results.tile([P, BATCH], F32, tag="h_new", name="h_new%d" % t, bufs=4)
             for part in parts_of(OUTPUT * TILES + t):
-                nc.scalar.activation(out=h_new[t][:, part], in_=wave_of[OUTPUT * TILES + t][:, part], func=ACT.Sigmoid, bias=column(bias[:, OUTPUT, :], t), scale=1.0)
+                nc.scalar.activation(out=h_new[t][:, part], in_=wave_of[OUTPUT * TILES + t][:, part], func=ACT.Sigmoid, bias=column(bias_bf[:, OUTPUT, :], t), scale=1.0)
 
         def v_h_new(t):
             for part in parts_of(OUTPUT * TILES + t):
@@ -264,7 +266,7 @@ def tile_slstmcell_pa_kernel(
             nc.scalar.activation(out=inv_n1[j][:], in_=inv_n1[j][:], func=ACT.Sigmoid, scale=-1.0)
 
         def s_edge():
-            nc.scalar.activation(out=edge[:], in_=edge[:], func=ACT.Sigmoid, scale=1.0)
+            nc.scalar.activation(out=edge[:], in_=bias_bf[:, FORGET, 0:TILES], func=ACT.Sigmoid, bias=floor[:], scale=1.0)
 
         def s_logs(j):
             if j == 0:
@@ -330,7 +332,6 @@ def tile_slstmcell_pa_kernel(
         evacuate(0, 1, nc.scalar.copy)
         regroup_moving(1)
         quantise(0)
-        make_constants()
         quantise_moving(1)
         regroup_moving(2)
         turn(1)
@@ -349,24 +350,19 @@ def tile_slstmcell_pa_kernel(
 
             if s < UNITS:
                 multiply(s)
-            if s == 0:
-                turn(2)
-            if s + 3 < UNITS:
+            if s <= AHEAD_FROM:
+                turn(s + 2)
+            if AHEAD_FROM <= s < UNITS - 3:
                 turn(s + 3)
 
-            emptied = s + 2
-            if emptied < FIRST_SHARED or AT_LOGS + 2 <= emptied < LAST_SHARED:
-                vector_takes = (0, 1)
-            elif emptied < AT_LOGS + 2:
-                vector_takes = (1,)
-            else:
-                vector_takes = ()
+            emptied = [u for u in range(2, UNITS) if s == (u - 1 if u <= AHEAD_FROM + 2 else u - 2)]
 
             at(v_floor, s - AT_FORGET)
 
-            for m in range(2):
-                if emptied < UNITS and m not in vector_takes:
-                    evacuate(emptied, m, nc.scalar.copy)
+            for u in emptied:
+                if u >= SCALAR_EMPTIES:
+                    evacuate(u, 0, nc.scalar.copy)
+                    evacuate(u, 1, nc.scalar.copy)
             if s in (0, 1):
                 s_log_n(2 * s)
                 s_log_n(2 * s + 1)
@@ -383,6 +379,10 @@ def tile_slstmcell_pa_kernel(
             at_pair(s_keep, s - AT_GROW - 1)
             at_pair(s_squash, s - AT_H_WAVE - 1)
 
+            for u in emptied:
+                if u < SCALAR_EMPTIES:
+                    evacuate(u, 0, nc.vector.tensor_copy)
+                    evacuate(u, 1, nc.vector.tensor_copy)
             at(v_h_new, s - AT_OUTPUT - 1)
             if s + 1 < UNITS:
                 quantise(s + 1)
@@ -391,9 +391,6 @@ def tile_slstmcell_pa_kernel(
             at_pair(v_product, s - AT_PRODUCT)
             at_pair(v_rise, s - AT_INPUT - 2)
             at_pair(v_log_fm, s - AT_INPUT)
-            for m in range(2):
-                if emptied < UNITS and m in vector_takes:
-                    evacuate(emptied, m, nc.vector.tensor_copy)
             at_pair(v_total, s - AT_PRODUCT - 1)
             at_pair(v_c_new, s - AT_H_WAVE - 2)
             at(v_input, s - AT_INPUT)

@@ -42,6 +42,7 @@ AT_H_WAVE = AT_PRODUCT + 2
 FLOOR = -16.0
 TINY = 2.0**-100
 AHEAD_FROM = TILES - 1
+FIRST_SHARED = 6
 SCALAR_EMPTIES = 11
 CEILING = 80.0
 GROWTH_CEILING = math.exp(CEILING)
@@ -83,8 +84,8 @@ def tile_slstmcell_pa_kernel(
         for gate in range(GATES):
             nc.scalar.dma_start(out=bias_bf[:, gate, 0:TILES], in_=b_of[gate].rearrange("(p t) -> p t", t=TILES))
 
-        moving_codes = consts.tile([P, 2 * PASSES, BATCH], U32, name="moving_codes", align_bytes=64)
-        moving_scales = consts.tile([P, 2 * PASSES, BATCH], U8, name="moving_scales", align_bytes=64)
+        moving_codes = consts.tile([P, 2 * PASSES, BATCH], U32, name="moving_codes", align_bytes=256)
+        moving_scales = consts.tile([P, 2 * PASSES, BATCH], U8, name="moving_scales", align_bytes=256)
         m_old = consts.tile([P, TILES, BATCH], BF16, name="m_old")
         n_old = consts.tile([P, TILES, BATCH], BF16, name="n_old")
         c_old = consts.tile([P, TILES, BATCH], BF16, name="c_old")
@@ -129,8 +130,8 @@ def tile_slstmcell_pa_kernel(
         load_moving(3)
         load_rows(0, slice(1, 2))
         load_rows(1, slice(0, 2))
-        load_n(0)
         load_m(0)
+        load_n(0)
         load_n(1)
         load_rows(2, slice(0, 2))
         load_m(1)
@@ -140,7 +141,7 @@ def tile_slstmcell_pa_kernel(
         moving_grouped = []
 
         def regroup_moving(j):
-            grouped = grouped_pool.tile([P, BATCH, PACK], BF16, tag="grouped", name="moving_grouped%d" % j, align_bytes=64)
+            grouped = grouped_pool.tile([P, BATCH, PACK], BF16, tag="grouped", name="moving_grouped%d" % j, align_bytes=256)
             moving_grouped.append(grouped)
             for engine_copy, cols in ((nc.vector.tensor_copy, slice(0, VECTOR_COLUMNS)), (nc.scalar.copy, slice(VECTOR_COLUMNS, BATCH))):
                 engine_copy(
@@ -183,7 +184,7 @@ def tile_slstmcell_pa_kernel(
 
         def evacuate(u, m, engine_copy):
             if u not in grouped_of:
-                grouped_of[u] = grouped_pool.tile([P, 2 * FEATURES], BF16, tag="grouped", name="grouped%d" % u, align_bytes=64)
+                grouped_of[u] = grouped_pool.tile([P, 2 * FEATURES], BF16, tag="grouped", name="grouped%d" % u, align_bytes=256)
             words = grouped_of[u][:].bitcast(F32)[:, m * WORDS : (m + 1) * WORDS]
             engine_copy(
                 out=words.rearrange("p (g h u) -> p g h u", g=PASSES, u=2),
@@ -191,8 +192,8 @@ def tile_slstmcell_pa_kernel(
             )
 
         def quantise(u):
-            codes_of[u] = codes_pool.tile([P, 2 * PASSES * P], U32, tag="codes", name="codes%d" % u, align_bytes=64)
-            scales_of[u] = codes_pool.tile([P, 2 * PASSES * P], U8, tag="scales", name="scales%d" % u, align_bytes=64)
+            codes_of[u] = codes_pool.tile([P, 2 * PASSES * P], U32, tag="codes", name="codes%d" % u, align_bytes=256)
+            scales_of[u] = codes_pool.tile([P, 2 * PASSES * P], U8, tag="scales", name="scales%d" % u, align_bytes=256)
             nc.vector.quantize_mx(out=codes_of[u][:].bitcast(FP8X4), scales=scales_of[u][:], in_=grouped_of[u][:])
 
         def multiply(u):
@@ -325,6 +326,11 @@ def tile_slstmcell_pa_kernel(
             if 0 <= j < PAIRS:
                 step(j)
 
+        def empties(u, m):
+            if u >= SCALAR_EMPTIES or (u >= FIRST_SHARED and m == 0):
+                return "scalar"
+            return "vector"
+
         regroup_moving(0)
         turn(0)
         quantise_moving(0)
@@ -360,9 +366,9 @@ def tile_slstmcell_pa_kernel(
             at(v_floor, s - AT_FORGET)
 
             for u in emptied:
-                if u >= SCALAR_EMPTIES:
-                    evacuate(u, 0, nc.scalar.copy)
-                    evacuate(u, 1, nc.scalar.copy)
+                for m in range(2):
+                    if empties(u, m) == "scalar":
+                        evacuate(u, m, nc.scalar.copy)
             if s in (0, 1):
                 s_log_n(2 * s)
                 s_log_n(2 * s + 1)
@@ -380,9 +386,9 @@ def tile_slstmcell_pa_kernel(
             at_pair(s_squash, s - AT_H_WAVE - 1)
 
             for u in emptied:
-                if u < SCALAR_EMPTIES:
-                    evacuate(u, 0, nc.vector.tensor_copy)
-                    evacuate(u, 1, nc.vector.tensor_copy)
+                for m in range(2):
+                    if empties(u, m) == "vector":
+                        evacuate(u, m, nc.vector.tensor_copy)
             at(v_h_new, s - AT_OUTPUT - 1)
             if s + 1 < UNITS:
                 quantise(s + 1)

import math
from contextlib import ExitStack

import concourse.mybir as mybir
from concourse.masks import make_identity

F32 = mybir.dt.float32
BF16 = mybir.dt.bfloat16
U32 = mybir.dt.uint32
U8 = mybir.dt.uint8
FP8X4 = mybir.dt.float8_e4m3fn_x4
ACT = mybir.ActivationFunctionType
ALU = mybir.AluOpType
ET = mybir.EngineType

P = 128
FEATURES = 1024
BATCH = 512
TILES = FEATURES // P
PAIRS = TILES // 2
PACK = 4
PASSES = FEATURES // (P * PACK)
WORDS = FEATURES // 2
GATES = 4
FORGET, INPUT, CELL, OUTPUT = range(GATES)
UNITS = GATES * TILES

FLOPS = 2 * 2 * GATES * FEATURES * FEATURES * BATCH

AT_FORGET = FORGET * TILES + 1
AT_INPUT = INPUT * TILES + 1
AT_CELL = CELL * TILES + 1
AT_OUTPUT = OUTPUT * TILES + 1
AT_SIGMOID = 2
AT_INV_N1 = AT_SIGMOID + 1
AT_LOGS = AT_FORGET + TILES - 1
AT_GROW = AT_LOGS + PAIRS
AT_N_NEW = AT_GROW + 4
AT_PRODUCT = AT_CELL + 2
AT_H_WAVE = AT_PRODUCT + 2

FLOOR = -16.0
TINY = 2.0**-100
AHEAD_FROM = TILES - 1
FIRST_SHARED = 6
SCALAR_EMPTIES = 11
CEILING = 80.0
GROWTH_CEILING = math.exp(CEILING)

RAW_AHEAD = 10
VECTOR_COLUMNS = 336


def tile_slstmcell_pa_kernel(
    tc, x, h_prev, c_prev, n_prev, m_prev,
    w_input, w_forget, w_output, w_z, r_input, r_forget, r_output, r_z,
    b_input, b_forget, b_output, b_z,
    out_0, out_1, out_2, out_3,
):
    nc = tc.nc
    w_of = (w_forget, w_input, w_z, w_output)
    r_of = (r_forget, r_input, r_z, r_output)
    b_of = (b_forget, b_input, b_z, b_output)

    def by_tile(a):
        return a.rearrange("(p t) c -> p t c", t=TILES)

    h_out, c_out, n_out, m_out = by_tile(out_0), by_tile(out_1), by_tile(out_2), by_tile(out_3)

    with ExitStack() as ctx:
        ctx.enter_context(tc.manual_schedule(engines={ET.PE, ET.SP, ET.Activation}))
        consts = ctx.enter_context(tc.tile_pool(name="consts", bufs=1))
        raw_pool = ctx.enter_context(tc.tile_pool(name="raw", bufs=RAW_AHEAD))
        grouped_pool = ctx.enter_context(tc.tile_pool(name="grouped", bufs=3))
        codes_pool = ctx.enter_context(tc.tile_pool(name="codes", bufs=3))
        state = ctx.enter_context(tc.tile_pool(name="state", bufs=PAIRS))
        results = ctx.enter_context(tc.tile_pool(name="results", bufs=2))
        turned_pool = ctx.enter_context(tc.psum_pool(name="turned", bufs=4))
        wave_pool = ctx.enter_context(tc.psum_pool(name="waves", bufs=4))

        identity = consts.tile([P, P], F32, name="identity")
        make_identity(nc, identity[:])
        bias_bf = consts.tile([P, GATES, 2 * TILES], BF16, name="bias_bf")
        for gate in range(GATES):
            nc.scalar.dma_start(out=bias_bf[:, gate, 0:TILES], in_=b_of[gate].rearrange("(p t) -> p t", t=TILES))

        moving_codes = consts.tile([P, 2 * PASSES, BATCH], U32, name="moving_codes", align_bytes=256)
        moving_scales = consts.tile([P, 2 * PASSES, BATCH], U8, name="moving_scales", align_bytes=256)
        m_old = consts.tile([P, TILES, BATCH], BF16, name="m_old")
        n_old = consts.tile([P, TILES, BATCH], BF16, name="n_old")
        c_old = consts.tile([P, TILES, BATCH], BF16, name="c_old")

        raw_of = {}

        def load_rows(pair, rows):
            gate, first = divmod(2 * pair, TILES)
            for m, matrix in enumerate((w_of[gate], r_of[gate])):
                if (pair, m) not in raw_of:
                    raw_of[(pair, m)] = raw_pool.tile([P, 2, FEATURES], BF16, tag="raw", name="raw%d_%d" % (pair, m))
                nc.sync.dma_start(out=raw_of[(pair, m)][:, rows, :], in_=by_tile(matrix)[:, first + rows.start : first + rows.stop, :])

        def load_pair(pair):
            load_rows(pair, slice(0, 2))
            load_old(pair)

        def load_m(pair):
            nc.sync.dma_start(out=m_old[:, 2 * pair : 2 * pair + 2, :], in_=by_tile(m_prev)[:, 2 * pair : 2 * pair + 2, :])

        def load_old(pair):
            gate, first = divmod(2 * pair, TILES)
            if gate == FORGET and pair >= 3:
                load_m(pair)
            if pair == PAIRS + 1:
                nc.sync.dma_start(out=c_old[:], in_=by_tile(c_prev))

        moving_raw = {}

        def load_moving(j):
            source, g = ((x, h_prev)[j // PASSES], j % PASSES)
            moving_raw[j] = raw_pool.tile([P, PACK, BATCH], BF16, tag="raw", name="moving_raw%d" % j)
            nc.sync.dma_start(out=moving_raw[j][:], in_=source.rearrange("(g q t) b -> q g t b", g=PASSES, t=PACK)[:, g])

        def load_n(j):
            nc.sync.dma_start(out=n_old[:, 4 * j : 4 * j + 4, :], in_=by_tile(n_prev)[:, 4 * j : 4 * j + 4, :])

        load_moving(0)
        load_rows(0, slice(0, 1))
        load_moving(1)
        load_moving(2)
        load_moving(3)
        load_rows(0, slice(1, 2))
        load_rows(1, slice(0, 2))
        load_m(0)
        load_n(0)
        load_n(1)
        load_rows(2, slice(0, 2))
        load_m(1)
        load_m(2)
        pairs_at_first = (RAW_AHEAD - 2 * PASSES) // 2

        moving_grouped = []

        def regroup_moving(j):
            grouped = grouped_pool.tile([P, BATCH, PACK], BF16, tag="grouped", name="moving_grouped%d" % j, align_bytes=256)
            moving_grouped.append(grouped)
            for engine_copy, cols in ((nc.vector.tensor_copy, slice(0, VECTOR_COLUMNS)), (nc.scalar.copy, slice(VECTOR_COLUMNS, BATCH))):
                engine_copy(
                    out=grouped[:, cols, :].rearrange("p (c i) t -> p c t i", i=4),
                    in_=moving_raw[j][:, :, cols].rearrange("p t (c i) -> p c t i", i=4),
                )

        def quantise_moving(j):
            nc.vector.quantize_mx(
                out=moving_codes[:, j, :].bitcast(FP8X4),
                scales=moving_scales[:, j, :],
                in_=moving_grouped[j][:].rearrange("p b t -> p (b t)"),
            )

        def column(table, t):
            return table[:, t : t + 1]

        tiny = consts.tile([P, 1], F32, name="tiny")
        nc.gpsimd.memset(tiny[:], TINY)
        first_log = consts.tile([P, 1], F32, name="first_log")
        nc.scalar.activation(out=first_log[:], in_=tiny[:], func=ACT.Ln, bias=tiny[:], scale=1.0)
        floor = consts.tile([P, 1], F32, name="floor")
        nc.gpsimd.memset(floor[:], FLOOR)
        edge = consts.tile([P, TILES], F32, name="edge")

        banks_of, grouped_of, codes_of, scales_of, wave_of = {}, {}, {}, {}, {}

        def parts_of(u):
            n = 2 if u == UNITS - 1 else 1
            return [slice(i * BATCH // n, (i + 1) * BATCH // n) for i in range(n)]

        def turn(u):
            for m in range(2):
                words = raw_of[(u // 2, m)][:, u % 2, :].bitcast(F32)
                bank = turned_pool.tile([P, 2 * PASSES, P], F32, tag="turned", name="turned%d_%d" % (u, m))
                for c in range(2 * PASSES):
                    first = 2 * P * (c // 2) + c % 2
                    nc.tensor.transpose(bank[:, c, :], words[:, first : 2 * P * (c // 2 + 1) : 2], identity[:])
                banks_of[(u, m)] = bank

        def evacuate(u, m, engine_copy):
            if u not in grouped_of:
                grouped_of[u] = grouped_pool.tile([P, 2 * FEATURES], BF16, tag="grouped", name="grouped%d" % u, align_bytes=256)
            words = grouped_of[u][:].bitcast(F32)[:, m * WORDS : (m + 1) * WORDS]
            engine_copy(
                out=words.rearrange("p (g h u) -> p g h u", g=PASSES, u=2),
                in_=banks_of[(u, m)][:].rearrange("p (g u) h -> p g h u", u=2),
            )

        def quantise(u):
            codes_of[u] = codes_pool.tile([P, 2 * PASSES * P], U32, tag="codes", name="codes%d" % u, align_bytes=256)
            scales_of[u] = codes_pool.tile([P, 2 * PASSES * P], U8, tag="scales", name="scales%d" % u, align_bytes=256)
            nc.vector.quantize_mx(out=codes_of[u][:].bitcast(FP8X4), scales=scales_of[u][:], in_=grouped_of[u][:])

        def multiply(u):
            wave_of[u] = wave_pool.tile([P, BATCH], F32, tag="wave", name="wave%d" % u)
            for part in parts_of(u):
                for j in range(2 * PASSES):
                    cols = slice(j * P, (j + 1) * P)
                    nc.tensor.matmul_mx(
                        out=wave_of[u][:, part],
                        lhsT=codes_of[u][:, cols].bitcast(FP8X4),
                        lhsT_scale=scales_of[u][:, cols],
                        rhs=moving_codes[:, j, part].bitcast(FP8X4),
                        rhs_scale=moving_scales[:, j, part],
                        start=(j == 0),
                        stop=(j == 2 * PASSES - 1),
                    )

        log_f, log_fm, inv_n1, gap, rise, total, h_wave, h_new, m_new = ({} for k in range(9))

        def pair_tile(pool, tag, j):
            return pool.tile([P, 2, BATCH], F32, tag=tag, name="%s%d" % (tag, j))

        def rows(j):
            return slice(2 * j, 2 * j + 2)

        def s_forget(t):
            if t % 2 == 0:
                log_f[t // 2] = pair_tile(state, "log_f_gap", t // 2)
            nc.scalar.activation(out=log_f[t // 2][:, t % 2, :], in_=wave_of[t][:], func=ACT.Sigmoid, bias=column(bias_bf[:, FORGET, :], t), scale=1.0)

        def v_floor(t):
            if t % 2 == 0:
                log_fm[t // 2] = pair_tile(state, "log_fm_h", t // 2)
            nc.vector.scalar_tensor_tensor(
                out=log_fm[t // 2][:, t % 2, :], in0=wave_of[t][:], scalar=FLOOR, in1=m_old[:, t, :], op0=ALU.min, op1=ALU.add
            )

        def v_input(t):
            wave = wave_of[INPUT * TILES + t]
            if t % 2 == 0:
                gap[t // 2] = pair_tile(state, "log_f_gap", PAIRS + t // 2)
                m_new[t // 2] = pair_tile(results, "m_new", t // 2)
            for out, op1 in ((gap[t // 2], ALU.subtract), (m_new[t // 2], ALU.max)):
                nc.vector.scalar_tensor_tensor(
                    out=out[:, t % 2, :], in0=wave[:], scalar=column(bias_bf[:, INPUT, :], t), in1=log_fm[t // 2][:, t % 2, :],
                    op0=ALU.add, op1=op1,
                )
            if t % 2 == 1:
                nc.sync.dma_start(out=m_out[:, rows(t // 2), :], in_=m_new[t // 2][:])

        def s_cell(t):
            if t % 2 == 0:
                total[t // 2] = pair_tile(state, "total", t // 2)
            nc.scalar.activation(out=total[t // 2][:, t % 2, :], in_=wave_of[CELL * TILES + t][:], func=ACT.Tanh, bias=column(bias_bf[:, CELL, :], t), scale=1.0)

        def s_output(t):
            h_new[t] = results.tile([P, BATCH], F32, tag="h_new", name="h_new%d" % t, bufs=4)
            for part in parts_of(OUTPUT * TILES + t):
                nc.scalar.activation(out=h_new[t][:, part], in_=wave_of[OUTPUT * TILES + t][:, part], func=ACT.Sigmoid, bias=column(bias_bf[:, OUTPUT, :], t), scale=1.0)

        def v_h_new(t):
            for part in parts_of(OUTPUT * TILES + t):
                nc.vector.tensor_tensor(out=h_new[t][:, part], in0=h_new[t][:, part], in1=h_wave[t // 2][:, t % 2, part], op=ALU.mult)
                nc.sync.dma_start(out=h_out[:, t, part], in_=h_new[t][:, part])

        def s_log_n(j):
            inv_n1[j] = pair_tile(state, "inv_n1", j)
            nc.scalar.activation(out=inv_n1[j][:], in_=n_old[:, rows(j), :], func=ACT.Ln, bias=tiny[:], scale=1.0)

        def s_inv_n1(j):
            nc.scalar.activation(out=inv_n1[j][:], in_=inv_n1[j][:], func=ACT.Sigmoid, scale=-1.0)

        def s_edge():
            nc.scalar.activation(out=edge[:], in_=bias_bf[:, FORGET, 0:TILES], func=ACT.Sigmoid, bias=floor[:], scale=1.0)

        def s_logs(j):
            if j == 0:
                nc.scalar.activation(out=edge[:], in_=edge[:], func=ACT.Ln, scale=math.exp(-FLOOR))
            nc.scalar.activation(out=log_f[j][:], in_=log_f[j][:], func=ACT.Ln, scale=math.exp(-FLOOR))

        def v_log_fm(j):
            for t in (2 * j, 2 * j + 1):
                half = log_fm[j][:, t % 2, :]
                nc.vector.scalar_tensor_tensor(
                    out=half, in0=log_f[j][:, t % 2, :], scalar=column(edge, t), in1=half, op0=ALU.max, op1=ALU.add
                )

        def v_rise(j):
            rise[j] = pair_tile(state, "rise", j)
            nc.vector.tensor_scalar(out=rise[j][:], in0=gap[j][:], scalar1=0.0, scalar2=CEILING, op0=ALU.max, op1=ALU.min)

        def s_grow(j):
            nc.scalar.activation(out=gap[j][:], in_=gap[j][:], func=ACT.Exp, scale=1.0)

        def s_keep(j):
            nc.scalar.activation(out=rise[j][:], in_=rise[j][:], func=ACT.Exp, scale=-1.0)

        def v_n_new(j):
            n_new = pair_tile(results, "n_new", j)
            nc.vector.scalar_tensor_tensor(out=n_new[:], in0=n_old[:, rows(j), :], scalar=1.0, in1=rise[j][:], op0=ALU.add, op1=ALU.mult)
            nc.sync.dma_start(out=n_out[:, rows(j), :], in_=n_new[:])

        def v_product(j):
            nc.vector.scalar_tensor_tensor(out=total[j][:], in0=gap[j][:], scalar=GROWTH_CEILING, in1=total[j][:], op0=ALU.min, op1=ALU.mult)

        def v_total(j):
            nc.vector.tensor_tensor(out=total[j][:], in0=total[j][:], in1=c_old[:, rows(j), :], op=ALU.add)

        def v_h_wave(j):
            h_wave[j] = pair_tile(state, "log_fm_h", PAIRS + j)
            nc.vector.tensor_tensor(out=h_wave[j][:], in0=total[j][:], in1=inv_n1[j][:], op=ALU.mult)

        def v_c_new(j):
            c_new = pair_tile(results, "c_new", j)
            nc.vector.tensor_tensor(out=c_new[:], in0=total[j][:], in1=rise[j][:], op=ALU.mult)
            nc.sync.dma_start(out=c_out[:, rows(j), :], in_=c_new[:])

        def s_squash(j):
            nc.scalar.activation(out=h_wave[j][:], in_=h_wave[j][:], func=ACT.Tanh, scale=1.0)

        def at(step, t):
            if 0 <= t < TILES:
                step(t)

        def at_pair(step, t):
            if 0 <= t < TILES and t % 2 == 0:
                step(t // 2)

        def at_each_pair(step, j):
            if 0 <= j < PAIRS:
                step(j)

        def empties(u, m):
            if u >= SCALAR_EMPTIES or (u >= FIRST_SHARED and m == 0):
                return "scalar"
            return "vector"

        regroup_moving(0)
        turn(0)
        quantise_moving(0)
        evacuate(0, 0, nc.scalar.copy)
        evacuate(0, 1, nc.scalar.copy)
        regroup_moving(1)
        quantise(0)
        quantise_moving(1)
        regroup_moving(2)
        turn(1)
        quantise_moving(2)
        regroup_moving(3)
        evacuate(1, 0, nc.scalar.copy)
        quantise_moving(3)
        evacuate(1, 1, nc.scalar.copy)

        for s in range(UNITS + 2):
            if s == 0:
                for pair in range(pairs_at_first, RAW_AHEAD // 2 + 1):
                    load_pair(pair)
            elif s % 2 == 0 and s // 2 + RAW_AHEAD // 2 < UNITS // 2:
                load_pair(s // 2 + RAW_AHEAD // 2)

            if s < UNITS:
                multiply(s)
            if s <= AHEAD_FROM:
                turn(s + 2)
            if AHEAD_FROM <= s < UNITS - 3:
                turn(s + 3)

            emptied = [u for u in range(2, UNITS) if s == (u - 1 if u <= AHEAD_FROM + 2 else u - 2)]

            at(v_floor, s - AT_FORGET)

            for u in emptied:
                for m in range(2):
                    if empties(u, m) == "scalar":
                        evacuate(u, m, nc.scalar.copy)
            if s in (0, 1):
                s_log_n(2 * s)
                s_log_n(2 * s + 1)
            at_each_pair(s_inv_n1, s - AT_INV_N1)
            at(s_cell, s - AT_CELL)
            at(s_output, s - AT_OUTPUT)
            if s == AT_LOGS - 1:
                s_edge()
            for t in range(TILES):
                if s == max(t + AT_FORGET, AT_SIGMOID):
                    s_forget(t)
            at_each_pair(s_logs, s - AT_LOGS)
            at_pair(s_grow, s - AT_GROW)
            at_pair(s_keep, s - AT_GROW - 1)
            at_pair(s_squash, s - AT_H_WAVE - 1)

            for u in emptied:
                for m in range(2):
                    if empties(u, m) == "vector":
                        evacuate(u, m, nc.vector.tensor_copy)
            at(v_h_new, s - AT_OUTPUT - 1)
            if s + 1 < UNITS:
                quantise(s + 1)
            at_pair(v_n_new, s - AT_N_NEW)
            at_pair(v_h_wave, s - AT_H_WAVE)
            at_pair(v_product, s - AT_PRODUCT)
            at_pair(v_rise, s - AT_INPUT - 2)
            at_pair(v_log_fm, s - AT_INPUT)
            at_pair(v_total, s - AT_PRODUCT - 1)
            at_pair(v_c_new, s - AT_H_WAVE - 2)
            at(v_input, s - AT_INPUT)
